import numpy as np
import ml_dtypes


def mxq(x, axis, fmt="e4m3"):
    dtype, down = {"e4m3": (ml_dtypes.float8_e4m3fn, 7), "e5m2": (ml_dtypes.float8_e5m2, 14)}[fmt]
    v = np.moveaxis(np.asarray(x, np.float32).astype(ml_dtypes.bfloat16).astype(np.float64), axis, -1)
    blocks = v.reshape(v.shape[:-1] + (-1, 32))
    amax = np.abs(blocks).max(-1, keepdims=True)
    byte = np.maximum(np.where(amax > 0, np.frexp(amax)[1] - 1 + 127, 0) - down, 1)
    scale = np.exp2(byte - 127.0)
    codes = (blocks / scale).astype(np.float32).astype(dtype).astype(np.float64)
    return np.moveaxis((codes * scale).reshape(v.shape), -1, axis)


WIDE = False


def mx_kscale(k):
    if not WIDE:
        return np.ones(k)
    levels = np.array([10, -10, 5, -5, 0])
    a = np.random.permutation(np.resize(levels, k // 512 * 4)).reshape(k // 512, 4)
    idx = np.arange(k)
    return np.exp2(a[idx // 512, idx % 128 // 32])


BF16 = ml_dtypes.bfloat16


def bf(x):
    return np.asarray(x, np.float32).astype(BF16)


def f64(x):
    return np.asarray(x).astype(np.float64)


E, D, H, C = 64, 1024, 512, 128


def silu(v):
    return v / (1.0 + np.exp(-v))


def setup_inputs():
    s = mx_kscale(D)
    t = mx_kscale(H)
    return {
        "node_embed": bf(np.random.standard_normal((E, D)) * s),
        "x_edge_c": bf(np.random.standard_normal((E, H)) * t),
        "ori": bf(np.random.standard_normal((E, D)) * s),
        "W1": bf(np.random.standard_normal((D, H)) * 1.0 / np.sqrt(D) / s[:, None]),
        "b1": bf(np.random.standard_normal(H) * 0.3),
        "W2": bf(np.random.standard_normal((H, D)) * 1.5 / np.sqrt(H) / t[:, None]),
        "b2": bf(np.random.standard_normal(D) * 0.3),
        "edge_num": E,
    }


def reference(node_embed, x_edge_c, ori, W1, b1, W2, b2, edge_num):
    x = np.concatenate([f64(node_embed), f64(ori)], axis=0)
    h = silu((mxq(x, 1, "e4m3") @ mxq(f64(W1), 0, "e4m3")) + f64(b1))
    h = (h.reshape(2, edge_num, H) * f64(x_edge_c).reshape(1, edge_num, H)).reshape(-1, H)
    y = silu((mxq(h, 1, "e4m3") @ mxq(f64(W2), 0, "e4m3")) + f64(b2))
    y = y.reshape(2 * edge_num, -1, C)
    return y[:edge_num] + y[edge_num:]

@@ -1,0 +1,223 @@
+import concourse.mybir as mybir
+from concourse.masks import make_identity
+
+F32 = mybir.dt.float32
+BF16 = mybir.dt.bfloat16
+U32 = mybir.dt.uint32
+U8 = mybir.dt.uint8
+FP8X4 = mybir.dt.float8_e4m3fn_x4
+SILU = mybir.ActivationFunctionType.Silu
+ADD = mybir.AluOpType.add
+MULT = mybir.AluOpType.mult
+
+P = 128
+PACK = 4
+K_PASS = P * PACK
+E, D, H = 64, 1024, 512
+ROWS = 2 * E
+PASSES_1 = D // K_PASS
+CHUNKS_1 = H // P
+CHUNKS_2 = D // P
+PIECE = 512
+RUN = 4
+VECTOR_COLS = 320
+
+FLOPS = 2 * ROWS * D * H + 2 * ROWS * H * D
+
+
+def regroup(nc, grouped, raw):
+    nc.vector.tensor_copy(
+        out=grouped[:, 0:VECTOR_COLS, :].rearrange("p (c i) j -> p c j i", i=RUN),
+        in_=raw[:, :, 0:VECTOR_COLS].rearrange("p j (c i) -> p c j i", i=RUN),
+    )
+    nc.scalar.copy(
+        out=grouped[:, VECTOR_COLS:PIECE, :].rearrange("p (c i) j -> p c j i", i=RUN),
+        in_=raw[:, :, VECTOR_COLS:PIECE].rearrange("p j (c i) -> p c j i", i=RUN),
+    )
+
+
+def quantise(nc, codes, scales, grouped):
+    nc.vector.quantize_mx(out=codes.bitcast(FP8X4), scales=scales, in_=grouped)
+
+
+def tile_node_interaction_s_kernel(
+    tc, node_embed, x_edge_c, ori, W1, b1, W2, b2, edge_num, out
+):
+    nc = tc.nc
+    assert edge_num == E
+
+    with tc.tile_pool(name="sbuf", bufs=1) as sbuf, tc.psum_pool(name="psum", bufs=8) as psum:
+        x_sb = sbuf.tile([P, 2, K_PASS], BF16)
+        for half, x_half in enumerate((node_embed, ori)):
+            nc.sync.dma_start(
+                out=x_sb[:, half, :], in_=x_half.rearrange("e (g k) -> (e g) k", g=PASSES_1)
+            )
+        w1_raw = sbuf.tile([P, PASSES_1, PACK, H], BF16)
+        w1_rows = W1.rearrange("(g p j) c -> g p j c", g=PASSES_1, j=PACK)
+        for g in range(PASSES_1):
+            nc.sync.dma_start(out=w1_raw[:, g], in_=w1_rows[g])
+        w2_raw = sbuf.tile([P, PACK, D], BF16)
+        w2_rows = W2.rearrange("(t p) n -> p t n", p=P)
+        for first in range(0, D, PIECE):
+            nc.sync.dma_start(
+                out=w2_raw[:, :, first : first + PIECE], in_=w2_rows[:, :, first : first + PIECE]
+            )
+        gate_sb = sbuf.tile([P, H // 2], BF16)
+        nc.scalar.dma_start(out=gate_sb[:], in_=x_edge_c.rearrange("e (s f) -> (e s) f", s=2))
+        bias_rows = sbuf.tile([P, P], BF16)
+        nc.vector.memset(bias_rows[:], 0.0)
+        nc.scalar.dma_start(out=bias_rows[0:CHUNKS_1, :], in_=b1.rearrange("(c p) -> c p", p=P))
+        nc.scalar.dma_start(
+            out=bias_rows[CHUNKS_1 : CHUNKS_1 + CHUNKS_2, :], in_=b2.rearrange("(c p) -> c p", p=P)
+        )
+
+        ident_f32 = sbuf.tile([P, P], F32)
+        make_identity(nc, ident_f32[:])
+        ident_bf16 = sbuf.tile([P, P], BF16)
+        make_identity(nc, ident_bf16[:])
+        warm = sbuf.tile([P, 1], F32)
+        nc.vector.memset(warm[:], 0.0)
+        nc.scalar.activation(out=warm[:], in_=warm[:], func=SILU)
+
+        x_grouped = sbuf.tile([P, PASSES_1 * ROWS * PACK], BF16, align_bytes=64)
+        x_grouped_words = x_grouped[:].bitcast(F32).rearrange(
+            "p (g half e u) -> p half g e u", g=PASSES_1, half=2, u=2
+        )
+        x_words = x_sb[:].bitcast(F32).rearrange("q half (p u) -> q half u p", u=2)
+        for half, copy in enumerate((nc.scalar.copy, nc.vector.tensor_copy)):
+            xt_ps = psum.tile([P, 2, E, PASSES_1], F32, tag="bank")
+            for u in range(2):
+                nc.tensor.transpose(
+                    xt_ps[:, u].rearrange("p e g -> p (e g)"), x_words[:, half, u, :], ident_f32[:]
+                )
+            copy(out=x_grouped_words[:, half], in_=xt_ps[:].rearrange("p u e g -> p g e u"))
+        x_codes = sbuf.tile([P, PASSES_1, ROWS], U32, align_bytes=64)
+        x_scales = sbuf.tile([P, PASSES_1, ROWS], U8, align_bytes=64)
+
+        gate_ps = psum.tile([P, 2, E, 2], BF16, tag="bank")
+        for b in range(2):
+            nc.tensor.transpose(
+                gate_ps[:, b].rearrange("p e s -> p (e s)"),
+                gate_sb[:, b * P : (b + 1) * P],
+                ident_bf16[:],
+            )
+        bias_ps = psum.tile([P, P], BF16, tag="bank")
+        nc.tensor.transpose(bias_ps[:], bias_rows[:], ident_bf16[:])
+
+        w1_grouped = sbuf.tile([P, PASSES_1, H, PACK], BF16, align_bytes=64)
+        w1_codes = sbuf.tile([P, PASSES_1, H], U32, align_bytes=64)
+        w1_scales = sbuf.tile([P, PASSES_1, H], U8, align_bytes=64)
+        w2_grouped = sbuf.tile([P, D, PACK], BF16, align_bytes=64)
+        w2_codes = sbuf.tile([P, D], U32, align_bytes=64)
+        w2_scales = sbuf.tile([P, D], U8, align_bytes=64)
+
+        def quantise_w1(g):
+            quantise(
+                nc, w1_codes[:, g], w1_scales[:, g], w1_grouped[:, g].rearrange("p w j -> p (w j)")
+            )
+
+        def regroup_w2(first):
+            regroup(
+                nc, w2_grouped[:, first : first + PIECE, :], w2_raw[:, :, first : first + PIECE]
+            )
+
+        def quantise_w2(first):
+            quantise(
+                nc,
+                w2_codes[:, first : first + PIECE],
+                w2_scales[:, first : first + PIECE],
+                w2_grouped[:, first : first + PIECE, :].rearrange("p w j -> p (w j)"),
+            )
+
+        a_ps = [psum.tile([P, ROWS], F32, tag="bank", name="a_ps%d" % c) for c in range(CHUNKS_1)]
+
+        def layer_1_pass(g):
+            for c in range(CHUNKS_1):
+                nc.tensor.matmul_mx(
+                    out=a_ps[c][:],
+                    lhsT=w1_codes[:, g, c * P : (c + 1) * P].bitcast(FP8X4),
+                    lhsT_scale=w1_scales[:, g, c * P : (c + 1) * P],
+                    rhs=x_codes[:, g, :].bitcast(FP8X4),
+                    rhs_scale=x_scales[:, g, :],
+                    start=(g == 0),
+                    stop=(g == PASSES_1 - 1),
+                )
+
+        regroup(nc, w1_grouped[:, 0], w1_raw[:, 0])
+        quantise(
+            nc,
+            x_codes[:].rearrange("p g r -> p (g r)"),
+            x_scales[:].rearrange("p g r -> p (g r)"),
+            x_grouped[:],
+        )
+        regroup(nc, w1_grouped[:, 1], w1_raw[:, 1])
+        gate_t = sbuf.tile([P, E, CHUNKS_1], BF16)
+        nc.scalar.copy(
+            out=gate_t[:].rearrange("p e (s b) -> p e s b", b=2),
+            in_=gate_ps[:].rearrange("p b e s -> p e s b"),
+        )
+        bias_t = sbuf.tile([P, CHUNKS_1 + CHUNKS_2], F32)
+        nc.scalar.copy(out=bias_t[:], in_=bias_ps[:, 0 : CHUNKS_1 + CHUNKS_2])
+        quantise_w1(0)
+        layer_1_pass(0)
+        regroup_w2(0)
+        quantise_w1(1)
+        layer_1_pass(1)
+
+        a_t = sbuf.tile([P, CHUNKS_1, ROWS], F32)
+        for c in range(CHUNKS_1):
+            nc.scalar.activation(
+                out=a_t[:, c, :], in_=a_ps[c][:], func=SILU, bias=bias_t[:, c : c + 1], scale=1.0
+            )
+        regroup_w2(PIECE)
+        quantise_w2(0)
+        h_grouped = sbuf.tile([P, ROWS * PACK], BF16, align_bytes=64)
+        nc.vector.tensor_tensor(
+            out=h_grouped[:].rearrange("p (half e c) -> p half e c", half=2, c=CHUNKS_1),
+            in0=a_t[:].rearrange("p c (half e) -> p half e c", half=2),
+            in1=gate_t[:].unsqueeze(1).to_broadcast([P, 2, E, CHUNKS_1]),
+            op=MULT,
+        )
+        h_codes = sbuf.tile([P, ROWS], U32, align_bytes=64)
+        h_scales = sbuf.tile([P, ROWS], U8, align_bytes=64)
+        quantise(nc, h_codes[:], h_scales[:], h_grouped[:])
+        quantise_w2(PIECE)
+
+        y_t = sbuf.tile([P, CHUNKS_2, ROWS], F32)
+        sum_t = sbuf.tile([P, CHUNKS_2, E], F32)
+        out_sb = sbuf.tile([P, CHUNKS_2 // 2, P], F32)
+        out_rows = out.rearrange("e (pair i) d -> i e pair d", i=2)
+        for pair in range(CHUNKS_2 // 2):
+            for c in (2 * pair, 2 * pair + 1):
+                y_ps = psum.tile([P, ROWS], F32, tag="bank")
+                nc.tensor.matmul_mx(
+                    out=y_ps[:],
+                    lhsT=w2_codes[:, c * P : (c + 1) * P].bitcast(FP8X4),
+                    lhsT_scale=w2_scales[:, c * P : (c + 1) * P],
+                    rhs=h_codes[:].bitcast(FP8X4),
+                    rhs_scale=h_scales[:],
+                    start=True,
+                    stop=True,
+                )
+                nc.scalar.activation(
+                    out=y_t[:, c, :],
+                    in_=y_ps[:],
+                    func=SILU,
+                    bias=bias_t[:, CHUNKS_1 + c : CHUNKS_1 + c + 1],
+                    scale=1.0,
+                )
+            both = slice(2 * pair, 2 * pair + 2)
+            nc.vector.tensor_tensor(
+                out=sum_t[:, both, :], in0=y_t[:, both, 0:E], in1=y_t[:, both, E:ROWS], op=ADD
+            )
+            out_ps = psum.tile([P, P], F32, tag="bank")
+            nc.tensor.transpose(
+                out_ps[:], sum_t[:, both, :].rearrange("p c e -> p (c e)"), ident_f32[:]
+            )
+            nc.vector.tensor_copy(out=out_sb[:, pair, :], in_=out_ps[:])
+            if pair % 2 == 1:
+                done = slice(pair - 1, pair + 1)
+                for i in range(2):
+                    nc.sync.dma_start(
+                        out=out_rows[i][:, done, :], in_=out_sb[i * E : (i + 1) * E, done, :]
+                    )

@@ -18,9 +18,10 @@ ROWS = 2 * E
 PASSES_1 = D // K_PASS
 CHUNKS_1 = H // P
 CHUNKS_2 = D // P
+PAIRS = CHUNKS_2 // 2
 PIECE = 512
 RUN = 4
-VECTOR_COLS = 320
+VECTOR_COLS = 256
 
 FLOPS = 2 * ROWS * D * H + 2 * ROWS * H * D
 
@@ -46,16 +47,18 @@ def tile_node_interaction_s_kernel(
     nc = tc.nc
     assert edge_num == E
 
-    with tc.tile_pool(name="sbuf", bufs=1) as sbuf, tc.psum_pool(name="psum", bufs=8) as psum:
+    with tc.tile_pool(name="sbuf", bufs=1) as sbuf, tc.psum_pool(
+        name="psum", bufs=8
+    ) as psum, tc.manual_schedule():
+        w1_raw = sbuf.tile([P, PASSES_1, PACK, H], BF16)
+        w1_rows = W1.rearrange("(g p j) c -> g p j c", g=PASSES_1, j=PACK)
+        nc.sync.dma_start(out=w1_raw[:, 0], in_=w1_rows[0])
         x_sb = sbuf.tile([P, 2, K_PASS], BF16)
         for half, x_half in enumerate((node_embed, ori)):
             nc.sync.dma_start(
                 out=x_sb[:, half, :], in_=x_half.rearrange("e (g k) -> (e g) k", g=PASSES_1)
             )
-        w1_raw = sbuf.tile([P, PASSES_1, PACK, H], BF16)
-        w1_rows = W1.rearrange("(g p j) c -> g p j c", g=PASSES_1, j=PACK)
-        for g in range(PASSES_1):
-            nc.sync.dma_start(out=w1_raw[:, g], in_=w1_rows[g])
+        nc.sync.dma_start(out=w1_raw[:, 1], in_=w1_rows[1])
         w2_raw = sbuf.tile([P, PACK, D], BF16)
         w2_rows = W2.rearrange("(t p) n -> p t n", p=P)
         for first in range(0, D, PIECE):
@@ -78,6 +81,36 @@ def tile_node_interaction_s_kernel(
         warm = sbuf.tile([P, 1], F32)
         nc.vector.memset(warm[:], 0.0)
         nc.scalar.activation(out=warm[:], in_=warm[:], func=SILU)
+
+        w1_grouped = sbuf.tile([P, PASSES_1, H, PACK], BF16, align_bytes=64)
+        w1_codes = sbuf.tile([P, PASSES_1, H], U32, align_bytes=64)
+        w1_scales = sbuf.tile([P, PASSES_1, H], U8, align_bytes=64)
+        w2_grouped = sbuf.tile([P, D, PACK], BF16, align_bytes=64)
+        w2_codes = sbuf.tile([P, D], U32, align_bytes=64)
+        w2_scales = sbuf.tile([P, D], U8, align_bytes=64)
+
+        def regroup_w1(g):
+            regroup(nc, w1_grouped[:, g], w1_raw[:, g])
+
+        def quantise_w1(g):
+            quantise(
+                nc, w1_codes[:, g], w1_scales[:, g], w1_grouped[:, g].rearrange("p w j -> p (w j)")
+            )
+
+        def regroup_w2(first):
+            regroup(
+                nc, w2_grouped[:, first : first + PIECE, :], w2_raw[:, :, first : first + PIECE]
+            )
+
+        def quantise_w2(first):
+            quantise(
+                nc,
+                w2_codes[:, first : first + PIECE],
+                w2_scales[:, first : first + PIECE],
+                w2_grouped[:, first : first + PIECE, :].rearrange("p w j -> p (w j)"),
+            )
+
+        regroup_w1(0)
 
         x_grouped = sbuf.tile([P, PASSES_1 * ROWS * PACK], BF16, align_bytes=64)
         x_grouped_words = x_grouped[:].bitcast(F32).rearrange(
@@ -104,31 +137,6 @@ def tile_node_interaction_s_kernel(
         bias_ps = psum.tile([P, P], BF16, tag="bank")
         nc.tensor.transpose(bias_ps[:], bias_rows[:], ident_bf16[:])
 
-        w1_grouped = sbuf.tile([P, PASSES_1, H, PACK], BF16, align_bytes=64)
-        w1_codes = sbuf.tile([P, PASSES_1, H], U32, align_bytes=64)
-        w1_scales = sbuf.tile([P, PASSES_1, H], U8, align_bytes=64)
-        w2_grouped = sbuf.tile([P, D, PACK], BF16, align_bytes=64)
-        w2_codes = sbuf.tile([P, D], U32, align_bytes=64)
-        w2_scales = sbuf.tile([P, D], U8, align_bytes=64)
-
-        def quantise_w1(g):
-            quantise(
-                nc, w1_codes[:, g], w1_scales[:, g], w1_grouped[:, g].rearrange("p w j -> p (w j)")
-            )
-
-        def regroup_w2(first):
-            regroup(
-                nc, w2_grouped[:, first : first + PIECE, :], w2_raw[:, :, first : first + PIECE]
-            )
-
-        def quantise_w2(first):
-            quantise(
-                nc,
-                w2_codes[:, first : first + PIECE],
-                w2_scales[:, first : first + PIECE],
-                w2_grouped[:, first : first + PIECE, :].rearrange("p w j -> p (w j)"),
-            )
-
         a_ps = [psum.tile([P, ROWS], F32, tag="bank", name="a_ps%d" % c) for c in range(CHUNKS_1)]
 
         def layer_1_pass(g):
@@ -143,14 +151,15 @@ def tile_node_interaction_s_kernel(
                     stop=(g == PASSES_1 - 1),
                 )
 
-        regroup(nc, w1_grouped[:, 0], w1_raw[:, 0])
+        quantise_w1(0)
         quantise(
             nc,
             x_codes[:].rearrange("p g r -> p (g r)"),
             x_scales[:].rearrange("p g r -> p (g r)"),
             x_grouped[:],
         )
-        regroup(nc, w1_grouped[:, 1], w1_raw[:, 1])
+        layer_1_pass(0)
+        regroup_w1(1)
         gate_t = sbuf.tile([P, E, CHUNKS_1], BF16)
         nc.scalar.copy(
             out=gate_t[:].rearrange("p e (s b) -> p e s b", b=2),
@@ -158,8 +167,6 @@ def tile_node_interaction_s_kernel(
         )
         bias_t = sbuf.tile([P, CHUNKS_1 + CHUNKS_2], F32)
         nc.scalar.copy(out=bias_t[:], in_=bias_ps[:, 0 : CHUNKS_1 + CHUNKS_2])
-        quantise_w1(0)
-        layer_1_pass(0)
         regroup_w2(0)
         quantise_w1(1)
         layer_1_pass(1)
@@ -184,28 +191,30 @@ def tile_node_interaction_s_kernel(
         quantise_w2(PIECE)
 
         y_t = sbuf.tile([P, CHUNKS_2, ROWS], F32)
+        for c in range(CHUNKS_2):
+            y_ps = psum.tile([P, ROWS], F32, tag="bank")
+            nc.tensor.matmul_mx(
+                out=y_ps[:],
+                lhsT=w2_codes[:, c * P : (c + 1) * P].bitcast(FP8X4),
+                lhsT_scale=w2_scales[:, c * P : (c + 1) * P],
+                rhs=h_codes[:].bitcast(FP8X4),
+                rhs_scale=h_scales[:],
+                start=True,
+                stop=True,
+            )
+            nc.scalar.activation(
+                out=y_t[:, c, :],
+                in_=y_ps[:],
+                func=SILU,
+                bias=bias_t[:, CHUNKS_1 + c : CHUNKS_1 + c + 1],
+                scale=1.0,
+            )
+
         sum_t = sbuf.tile([P, CHUNKS_2, E], F32)
-        out_sb = sbuf.tile([P, CHUNKS_2 // 2, P], F32)
+        out_sb = sbuf.tile([P, PAIRS, P], F32)
         out_rows = out.rearrange("e (pair i) d -> i e pair d", i=2)
-        for pair in range(CHUNKS_2 // 2):
-            for c in (2 * pair, 2 * pair + 1):
-                y_ps = psum.tile([P, ROWS], F32, tag="bank")
-                nc.tensor.matmul_mx(
-                    out=y_ps[:],
-                    lhsT=w2_codes[:, c * P : (c + 1) * P].bitcast(FP8X4),
-                    lhsT_scale=w2_scales[:, c * P : (c + 1) * P],
-                    rhs=h_codes[:].bitcast(FP8X4),
-                    rhs_scale=h_scales[:],
-                    start=True,
-                    stop=True,
-                )
-                nc.scalar.activation(
-                    out=y_t[:, c, :],
-                    in_=y_ps[:],
-                    func=SILU,
-                    bias=bias_t[:, CHUNKS_1 + c : CHUNKS_1 + c + 1],
-                    scale=1.0,
-                )
+
+        def fold(pair):
             both = slice(2 * pair, 2 * pair + 2)
             nc.vector.tensor_tensor(
                 out=sum_t[:, both, :], in0=y_t[:, both, 0:E], in1=y_t[:, both, E:ROWS], op=ADD
@@ -214,6 +223,9 @@ def tile_node_interaction_s_kernel(
             nc.tensor.transpose(
                 out_ps[:], sum_t[:, both, :].rearrange("p c e -> p (c e)"), ident_f32[:]
             )
+            return out_ps
+
+        def finish(pair, out_ps):
             nc.vector.tensor_copy(out=out_sb[:, pair, :], in_=out_ps[:])
             if pair % 2 == 1:
                 done = slice(pair - 1, pair + 1)
@@ -221,3 +233,10 @@ def tile_node_interaction_s_kernel(
                     nc.sync.dma_start(
                         out=out_rows[i][:, done, :], in_=out_sb[i * E : (i + 1) * E, done, :]
                     )
+
+        folded = fold(0)
+        for pair in range(1, PAIRS):
+            folded_next = fold(pair)
+            finish(pair - 1, folded)
+            folded = folded_next
+        finish(PAIRS - 1, folded)

@@ -7,7 +7,6 @@ U32 = mybir.dt.uint32
 U8 = mybir.dt.uint8
 FP8X4 = mybir.dt.float8_e4m3fn_x4
 SILU = mybir.ActivationFunctionType.Silu
-ADD = mybir.AluOpType.add
 MULT = mybir.AluOpType.mult
 
 P = 128
@@ -21,7 +20,7 @@ CHUNKS_2 = D // P
 PAIRS = CHUNKS_2 // 2
 PIECE = 512
 RUN = 4
-VECTOR_COLS = 256
+VECTOR_COLS = 288
 
 FLOPS = 2 * ROWS * D * H + 2 * ROWS * H * D
 
@@ -50,15 +49,15 @@ def tile_node_interaction_s_kernel(
     with tc.tile_pool(name="sbuf", bufs=1) as sbuf, tc.psum_pool(
         name="psum", bufs=8
     ) as psum, tc.manual_schedule():
-        w1_raw = sbuf.tile([P, PASSES_1, PACK, H], BF16)
-        w1_rows = W1.rearrange("(g p j) c -> g p j c", g=PASSES_1, j=PACK)
-        nc.sync.dma_start(out=w1_raw[:, 0], in_=w1_rows[0])
         x_sb = sbuf.tile([P, 2, K_PASS], BF16)
         for half, x_half in enumerate((node_embed, ori)):
             nc.sync.dma_start(
                 out=x_sb[:, half, :], in_=x_half.rearrange("e (g k) -> (e g) k", g=PASSES_1)
             )
-        nc.sync.dma_start(out=w1_raw[:, 1], in_=w1_rows[1])
+        w1_raw = sbuf.tile([P, PASSES_1, PACK, H], BF16)
+        w1_rows = W1.rearrange("(g p j) c -> g p j c", g=PASSES_1, j=PACK)
+        for g in range(PASSES_1):
+            nc.sync.dma_start(out=w1_raw[:, g], in_=w1_rows[g])
         w2_raw = sbuf.tile([P, PACK, D], BF16)
         w2_rows = W2.rearrange("(t p) n -> p t n", p=P)
         for first in range(0, D, PIECE):
@@ -82,36 +81,6 @@ def tile_node_interaction_s_kernel(
         nc.vector.memset(warm[:], 0.0)
         nc.scalar.activation(out=warm[:], in_=warm[:], func=SILU)
 
-        w1_grouped = sbuf.tile([P, PASSES_1, H, PACK], BF16, align_bytes=64)
-        w1_codes = sbuf.tile([P, PASSES_1, H], U32, align_bytes=64)
-        w1_scales = sbuf.tile([P, PASSES_1, H], U8, align_bytes=64)
-        w2_grouped = sbuf.tile([P, D, PACK], BF16, align_bytes=64)
-        w2_codes = sbuf.tile([P, D], U32, align_bytes=64)
-        w2_scales = sbuf.tile([P, D], U8, align_bytes=64)
-
-        def regroup_w1(g):
-            regroup(nc, w1_grouped[:, g], w1_raw[:, g])
-
-        def quantise_w1(g):
-            quantise(
-                nc, w1_codes[:, g], w1_scales[:, g], w1_grouped[:, g].rearrange("p w j -> p (w j)")
-            )
-
-        def regroup_w2(first):
-            regroup(
-                nc, w2_grouped[:, first : first + PIECE, :], w2_raw[:, :, first : first + PIECE]
-            )
-
-        def quantise_w2(first):
-            quantise(
-                nc,
-                w2_codes[:, first : first + PIECE],
-                w2_scales[:, first : first + PIECE],
-                w2_grouped[:, first : first + PIECE, :].rearrange("p w j -> p (w j)"),
-            )
-
-        regroup_w1(0)
-
         x_grouped = sbuf.tile([P, PASSES_1 * ROWS * PACK], BF16, align_bytes=64)
         x_grouped_words = x_grouped[:].bitcast(F32).rearrange(
             "p (g half e u) -> p half g e u", g=PASSES_1, half=2, u=2
@@ -126,6 +95,12 @@ def tile_node_interaction_s_kernel(
             copy(out=x_grouped_words[:, half], in_=xt_ps[:].rearrange("p u e g -> p g e u"))
         x_codes = sbuf.tile([P, PASSES_1, ROWS], U32, align_bytes=64)
         x_scales = sbuf.tile([P, PASSES_1, ROWS], U8, align_bytes=64)
+        quantise(
+            nc,
+            x_codes[:].rearrange("p g r -> p (g r)"),
+            x_scales[:].rearrange("p g r -> p (g r)"),
+            x_grouped[:],
+        )
 
         gate_ps = psum.tile([P, 2, E, 2], BF16, tag="bank")
         for b in range(2):
@@ -137,9 +112,16 @@ def tile_node_interaction_s_kernel(
         bias_ps = psum.tile([P, P], BF16, tag="bank")
         nc.tensor.transpose(bias_ps[:], bias_rows[:], ident_bf16[:])
 
+        w1_grouped = sbuf.tile([P, PASSES_1, H, PACK], BF16, align_bytes=64)
+        w1_codes = sbuf.tile([P, PASSES_1, H], U32, align_bytes=64)
+        w1_scales = sbuf.tile([P, PASSES_1, H], U8, align_bytes=64)
         a_ps = [psum.tile([P, ROWS], F32, tag="bank", name="a_ps%d" % c) for c in range(CHUNKS_1)]
-
-        def layer_1_pass(g):
+        for g in range(PASSES_1):
+            regroup(nc, w1_grouped[:, g], w1_raw[:, g])
+        for g in range(PASSES_1):
+            quantise(
+                nc, w1_codes[:, g], w1_scales[:, g], w1_grouped[:, g].rearrange("p w j -> p (w j)")
+            )
             for c in range(CHUNKS_1):
                 nc.tensor.matmul_mx(
                     out=a_ps[c][:],
@@ -151,46 +133,47 @@ def tile_node_interaction_s_kernel(
                     stop=(g == PASSES_1 - 1),
                 )
 
-        quantise_w1(0)
-        quantise(
-            nc,
-            x_codes[:].rearrange("p g r -> p (g r)"),
-            x_scales[:].rearrange("p g r -> p (g r)"),
-            x_grouped[:],
-        )
-        layer_1_pass(0)
-        regroup_w1(1)
-        gate_t = sbuf.tile([P, E, CHUNKS_1], BF16)
-        nc.scalar.copy(
-            out=gate_t[:].rearrange("p e (s b) -> p e s b", b=2),
-            in_=gate_ps[:].rearrange("p b e s -> p e s b"),
-        )
+        w2_grouped = sbuf.tile([P, D, PACK], BF16, align_bytes=64)
+        w2_codes = sbuf.tile([P, D], U32, align_bytes=64)
+        w2_scales = sbuf.tile([P, D], U8, align_bytes=64)
+
+        def regroup_w2(first):
+            regroup(
+                nc, w2_grouped[:, first : first + PIECE, :], w2_raw[:, :, first : first + PIECE]
+            )
+
+        def quantise_w2(first):
+            quantise(
+                nc,
+                w2_codes[:, first : first + PIECE],
+                w2_scales[:, first : first + PIECE],
+                w2_grouped[:, first : first + PIECE, :].rearrange("p w j -> p (w j)"),
+            )
+
+        regroup_w2(0)
         bias_t = sbuf.tile([P, CHUNKS_1 + CHUNKS_2], F32)
         nc.scalar.copy(out=bias_t[:], in_=bias_ps[:, 0 : CHUNKS_1 + CHUNKS_2])
-        regroup_w2(0)
-        quantise_w1(1)
-        layer_1_pass(1)
-
         a_t = sbuf.tile([P, CHUNKS_1, ROWS], F32)
         for c in range(CHUNKS_1):
             nc.scalar.activation(
                 out=a_t[:, c, :], in_=a_ps[c][:], func=SILU, bias=bias_t[:, c : c + 1], scale=1.0
             )
-        regroup_w2(PIECE)
         quantise_w2(0)
-        h_grouped = sbuf.tile([P, ROWS * PACK], BF16, align_bytes=64)
-        nc.vector.tensor_tensor(
-            out=h_grouped[:].rearrange("p (half e c) -> p half e c", half=2, c=CHUNKS_1),
-            in0=a_t[:].rearrange("p c (half e) -> p half e c", half=2),
-            in1=gate_t[:].unsqueeze(1).to_broadcast([P, 2, E, CHUNKS_1]),
-            op=MULT,
-        )
+        h_grouped = sbuf.tile([P, 2, E * PACK], BF16, align_bytes=64)
+        for half in range(2):
+            nc.vector.tensor_tensor(
+                out=h_grouped[:, half, :].rearrange("p (e s b) -> p e s b", s=2, b=2),
+                in0=a_t[:, :, half * E : (half + 1) * E].rearrange("p (s b) e -> p e s b", b=2),
+                in1=gate_ps[:].rearrange("p b e s -> p e s b"),
+                op=MULT,
+            )
         h_codes = sbuf.tile([P, ROWS], U32, align_bytes=64)
         h_scales = sbuf.tile([P, ROWS], U8, align_bytes=64)
-        quantise(nc, h_codes[:], h_scales[:], h_grouped[:])
+        quantise(nc, h_codes[:], h_scales[:], h_grouped[:].rearrange("p half f -> p (half f)"))
+        regroup_w2(PIECE)
         quantise_w2(PIECE)
 
-        y_t = sbuf.tile([P, CHUNKS_2, ROWS], F32)
+        y_t = sbuf.tile([P, 2, CHUNKS_2, E], F32)
         for c in range(CHUNKS_2):
             y_ps = psum.tile([P, ROWS], F32, tag="bank")
             nc.tensor.matmul_mx(
@@ -203,29 +186,26 @@ def tile_node_interaction_s_kernel(
                 stop=True,
             )
             nc.scalar.activation(
-                out=y_t[:, c, :],
-                in_=y_ps[:],
+                out=y_t[:, :, c, :],
+                in_=y_ps[:].rearrange("p (half e) -> p half e", half=2),
                 func=SILU,
                 bias=bias_t[:, CHUNKS_1 + c : CHUNKS_1 + c + 1],
                 scale=1.0,
             )
 
-        sum_t = sbuf.tile([P, CHUNKS_2, E], F32)
         out_sb = sbuf.tile([P, PAIRS, P], F32)
         out_rows = out.rearrange("e (pair i) d -> i e pair d", i=2)
-
-        def fold(pair):
-            both = slice(2 * pair, 2 * pair + 2)
-            nc.vector.tensor_tensor(
-                out=sum_t[:, both, :], in0=y_t[:, both, 0:E], in1=y_t[:, both, E:ROWS], op=ADD
-            )
+        for pair in range(PAIRS):
             out_ps = psum.tile([P, P], F32, tag="bank")
-            nc.tensor.transpose(
-                out_ps[:], sum_t[:, both, :].rearrange("p c e -> p (c e)"), ident_f32[:]
-            )
-            return out_ps
-
-        def finish(pair, out_ps):
+            for half in range(2):
+                nc.tensor.matmul(
+                    out=out_ps[:],
+                    lhsT=y_t[:, half, 2 * pair : 2 * pair + 2, :].rearrange("p c e -> p (c e)"),
+                    rhs=ident_f32[:],
+                    start=(half == 0),
+                    stop=(half == 1),
+                    is_transpose=True,
+                )
             nc.vector.tensor_copy(out=out_sb[:, pair, :], in_=out_ps[:])
             if pair % 2 == 1:
                 done = slice(pair - 1, pair + 1)
@@ -233,10 +213,3 @@ def tile_node_interaction_s_kernel(
                     nc.sync.dma_start(
                         out=out_rows[i][:, done, :], in_=out_sb[i * E : (i + 1) * E, done, :]
                     )
-
-        folded = fold(0)
-        for pair in range(1, PAIRS):
-            folded_next = fold(pair)
-            finish(pair - 1, folded)
-            folded = folded_next
-        finish(PAIRS - 1, folded)

@@ -18,9 +18,10 @@ PASSES_1 = D // K_PASS
 CHUNKS_1 = H // P
 CHUNKS_2 = D // P
 PAIRS = CHUNKS_2 // 2
+LAG = 2
 PIECE = 512
 RUN = 4
-VECTOR_COLS = 288
+VECTOR_COLS = 256
 
 FLOPS = 2 * ROWS * D * H + 2 * ROWS * H * D
 
@@ -55,9 +56,11 @@ def tile_node_interaction_s_kernel(
                 out=x_sb[:, half, :], in_=x_half.rearrange("e (g k) -> (e g) k", g=PASSES_1)
             )
         w1_raw = sbuf.tile([P, PASSES_1, PACK, H], BF16)
-        w1_rows = W1.rearrange("(g p j) c -> g p j c", g=PASSES_1, j=PACK)
+        w1_rows = W1.rearrange("(g u p v) c -> g p u (v c)", g=PASSES_1, u=2, v=2)
         for g in range(PASSES_1):
-            nc.sync.dma_start(out=w1_raw[:, g], in_=w1_rows[g])
+            nc.sync.dma_start(
+                out=w1_raw[:, g].rearrange("p (u v) c -> p u (v c)", u=2), in_=w1_rows[g]
+            )
         w2_raw = sbuf.tile([P, PACK, D], BF16)
         w2_rows = W2.rearrange("(t p) n -> p t n", p=P)
         for first in range(0, D, PIECE):
@@ -85,7 +88,7 @@ def tile_node_interaction_s_kernel(
         x_grouped_words = x_grouped[:].bitcast(F32).rearrange(
             "p (g half e u) -> p half g e u", g=PASSES_1, half=2, u=2
         )
-        x_words = x_sb[:].bitcast(F32).rearrange("q half (p u) -> q half u p", u=2)
+        x_words = x_sb[:].bitcast(F32).rearrange("q half (u p) -> q half u p", u=2)
         for half, copy in enumerate((nc.scalar.copy, nc.vector.tensor_copy)):
             xt_ps = psum.tile([P, 2, E, PASSES_1], F32, tag="bank")
             for u in range(2):
@@ -95,12 +98,6 @@ def tile_node_interaction_s_kernel(
             copy(out=x_grouped_words[:, half], in_=xt_ps[:].rearrange("p u e g -> p g e u"))
         x_codes = sbuf.tile([P, PASSES_1, ROWS], U32, align_bytes=64)
         x_scales = sbuf.tile([P, PASSES_1, ROWS], U8, align_bytes=64)
-        quantise(
-            nc,
-            x_codes[:].rearrange("p g r -> p (g r)"),
-            x_scales[:].rearrange("p g r -> p (g r)"),
-            x_grouped[:],
-        )
 
         gate_ps = psum.tile([P, 2, E, 2], BF16, tag="bank")
         for b in range(2):
@@ -116,8 +113,14 @@ def tile_node_interaction_s_kernel(
         w1_codes = sbuf.tile([P, PASSES_1, H], U32, align_bytes=64)
         w1_scales = sbuf.tile([P, PASSES_1, H], U8, align_bytes=64)
         a_ps = [psum.tile([P, ROWS], F32, tag="bank", name="a_ps%d" % c) for c in range(CHUNKS_1)]
-        for g in range(PASSES_1):
-            regroup(nc, w1_grouped[:, g], w1_raw[:, g])
+        regroup(nc, w1_grouped[:, 0], w1_raw[:, 0])
+        quantise(
+            nc,
+            x_codes[:].rearrange("p g r -> p (g r)"),
+            x_scales[:].rearrange("p g r -> p (g r)"),
+            x_grouped[:],
+        )
+        regroup(nc, w1_grouped[:, 1], w1_raw[:, 1])
         for g in range(PASSES_1):
             quantise(
                 nc, w1_codes[:, g], w1_scales[:, g], w1_grouped[:, g].rearrange("p w j -> p (w j)")
@@ -158,6 +161,7 @@ def tile_node_interaction_s_kernel(
             nc.scalar.activation(
                 out=a_t[:, c, :], in_=a_ps[c][:], func=SILU, bias=bias_t[:, c : c + 1], scale=1.0
             )
+        regroup_w2(PIECE)
         quantise_w2(0)
         h_grouped = sbuf.tile([P, 2, E * PACK], BF16, align_bytes=64)
         for half in range(2):
@@ -170,11 +174,11 @@ def tile_node_interaction_s_kernel(
         h_codes = sbuf.tile([P, ROWS], U32, align_bytes=64)
         h_scales = sbuf.tile([P, ROWS], U8, align_bytes=64)
         quantise(nc, h_codes[:], h_scales[:], h_grouped[:].rearrange("p half f -> p (half f)"))
-        regroup_w2(PIECE)
         quantise_w2(PIECE)
 
         y_t = sbuf.tile([P, 2, CHUNKS_2, E], F32)
-        for c in range(CHUNKS_2):
+
+        def layer_2_chunk(c):
             y_ps = psum.tile([P, ROWS], F32, tag="bank")
             nc.tensor.matmul_mx(
                 out=y_ps[:],
@@ -195,7 +199,8 @@ def tile_node_interaction_s_kernel(
 
         out_sb = sbuf.tile([P, PAIRS, P], F32)
         out_rows = out.rearrange("e (pair i) d -> i e pair d", i=2)
-        for pair in range(PAIRS):
+
+        def close_pair(pair):
             out_ps = psum.tile([P, P], F32, tag="bank")
             for half in range(2):
                 nc.tensor.matmul(
@@ -213,3 +218,10 @@ def tile_node_interaction_s_kernel(
                     nc.sync.dma_start(
                         out=out_rows[i][:, done, :], in_=out_sb[i * E : (i + 1) * E, done, :]
                     )
+
+        for step in range(PAIRS + LAG):
+            if step < PAIRS:
+                layer_2_chunk(2 * step)
+                layer_2_chunk(2 * step + 1)
+            if step >= LAG:
+                close_pair(step - LAG)

import concourse.mybir as mybir
from concourse.masks import make_identity

F32 = mybir.dt.float32
BF16 = mybir.dt.bfloat16
U32 = mybir.dt.uint32
U8 = mybir.dt.uint8
FP8X4 = mybir.dt.float8_e4m3fn_x4
SILU = mybir.ActivationFunctionType.Silu
MULT = mybir.AluOpType.mult

P = 128
PACK = 4
K_PASS = P * PACK
E, D, H = 64, 1024, 512
ROWS = 2 * E
PASSES_1 = D // K_PASS
CHUNKS_1 = H // P
CHUNKS_2 = D // P
PAIRS = CHUNKS_2 // 2
LAG = 2
PIECE = 512
RUN = 4
VECTOR_COLS = 256

FLOPS = 2 * ROWS * D * H + 2 * ROWS * H * D


def regroup(nc, grouped, raw):
    nc.vector.tensor_copy(
        out=grouped[:, 0:VECTOR_COLS, :].rearrange("p (c i) j -> p c j i", i=RUN),
        in_=raw[:, :, 0:VECTOR_COLS].rearrange("p j (c i) -> p c j i", i=RUN),
    )
    nc.scalar.copy(
        out=grouped[:, VECTOR_COLS:PIECE, :].rearrange("p (c i) j -> p c j i", i=RUN),
        in_=raw[:, :, VECTOR_COLS:PIECE].rearrange("p j (c i) -> p c j i", i=RUN),
    )


def quantise(nc, codes, scales, grouped):
    nc.vector.quantize_mx(out=codes.bitcast(FP8X4), scales=scales, in_=grouped)


def tile_node_interaction_s_kernel(
    tc, node_embed, x_edge_c, ori, W1, b1, W2, b2, edge_num, out
):
    nc = tc.nc
    assert edge_num == E

    with tc.tile_pool(name="sbuf", bufs=1) as sbuf, tc.psum_pool(
        name="psum", bufs=8
    ) as psum, tc.manual_schedule():
        x_sb = sbuf.tile([P, 2, K_PASS], BF16)
        for half, x_half in enumerate((node_embed, ori)):
            nc.sync.dma_start(
                out=x_sb[:, half, :], in_=x_half.rearrange("e (g k) -> (e g) k", g=PASSES_1)
            )
        w1_raw = sbuf.tile([P, PASSES_1, PACK, H], BF16)
        w1_rows = W1.rearrange("(g u p v) c -> g p u (v c)", g=PASSES_1, u=2, v=2)
        for g in range(PASSES_1):
            nc.sync.dma_start(
                out=w1_raw[:, g].rearrange("p (u v) c -> p u (v c)", u=2), in_=w1_rows[g]
            )
        w2_raw = sbuf.tile([P, PACK, D], BF16)
        w2_rows = W2.rearrange("(t p) n -> p t n", p=P)
        for first in range(0, D, PIECE):
            nc.sync.dma_start(
                out=w2_raw[:, :, first : first + PIECE], in_=w2_rows[:, :, first : first + PIECE]
            )
        gate_sb = sbuf.tile([P, H // 2], BF16)
        nc.scalar.dma_start(out=gate_sb[:], in_=x_edge_c.rearrange("e (s f) -> (e s) f", s=2))
        bias_rows = sbuf.tile([P, P], BF16)
        nc.vector.memset(bias_rows[:], 0.0)
        nc.scalar.dma_start(out=bias_rows[0:CHUNKS_1, :], in_=b1.rearrange("(c p) -> c p", p=P))
        nc.scalar.dma_start(
            out=bias_rows[CHUNKS_1 : CHUNKS_1 + CHUNKS_2, :], in_=b2.rearrange("(c p) -> c p", p=P)
        )

        ident_f32 = sbuf.tile([P, P], F32)
        make_identity(nc, ident_f32[:])
        ident_bf16 = sbuf.tile([P, P], BF16)
        make_identity(nc, ident_bf16[:])
        warm = sbuf.tile([P, 1], F32)
        nc.vector.memset(warm[:], 0.0)
        nc.scalar.activation(out=warm[:], in_=warm[:], func=SILU)

        x_grouped = sbuf.tile([P, PASSES_1 * ROWS * PACK], BF16, align_bytes=64)
        x_grouped_words = x_grouped[:].bitcast(F32).rearrange(
            "p (g half e u) -> p half g e u", g=PASSES_1, half=2, u=2
        )
        x_words = x_sb[:].bitcast(F32).rearrange("q half (u p) -> q half u p", u=2)
        for half, copy in enumerate((nc.scalar.copy, nc.vector.tensor_copy)):
            xt_ps = psum.tile([P, 2, E, PASSES_1], F32, tag="bank")
            for u in range(2):
                nc.tensor.transpose(
                    xt_ps[:, u].rearrange("p e g -> p (e g)"), x_words[:, half, u, :], ident_f32[:]
                )
            copy(out=x_grouped_words[:, half], in_=xt_ps[:].rearrange("p u e g -> p g e u"))
        x_codes = sbuf.tile([P, PASSES_1, ROWS], U32, align_bytes=64)
        x_scales = sbuf.tile([P, PASSES_1, ROWS], U8, align_bytes=64)

        gate_ps = psum.tile([P, 2, E, 2], BF16, tag="bank")
        for b in range(2):
            nc.tensor.transpose(
                gate_ps[:, b].rearrange("p e s -> p (e s)"),
                gate_sb[:, b * P : (b + 1) * P],
                ident_bf16[:],
            )
        bias_ps = psum.tile([P, P], BF16, tag="bank")
        nc.tensor.transpose(bias_ps[:], bias_rows[:], ident_bf16[:])

        w1_grouped = sbuf.tile([P, PASSES_1, H, PACK], BF16, align_bytes=64)
        w1_codes = sbuf.tile([P, PASSES_1, H], U32, align_bytes=64)
        w1_scales = sbuf.tile([P, PASSES_1, H], U8, align_bytes=64)
        a_ps = [psum.tile([P, ROWS], F32, tag="bank", name="a_ps%d" % c) for c in range(CHUNKS_1)]
        regroup(nc, w1_grouped[:, 0], w1_raw[:, 0])
        quantise(
            nc,
            x_codes[:].rearrange("p g r -> p (g r)"),
            x_scales[:].rearrange("p g r -> p (g r)"),
            x_grouped[:],
        )
        regroup(nc, w1_grouped[:, 1], w1_raw[:, 1])
        for g in range(PASSES_1):
            quantise(
                nc, w1_codes[:, g], w1_scales[:, g], w1_grouped[:, g].rearrange("p w j -> p (w j)")
            )
            for c in range(CHUNKS_1):
                nc.tensor.matmul_mx(
                    out=a_ps[c][:],
                    lhsT=w1_codes[:, g, c * P : (c + 1) * P].bitcast(FP8X4),
                    lhsT_scale=w1_scales[:, g, c * P : (c + 1) * P],
                    rhs=x_codes[:, g, :].bitcast(FP8X4),
                    rhs_scale=x_scales[:, g, :],
                    start=(g == 0),
                    stop=(g == PASSES_1 - 1),
                )

        w2_grouped = sbuf.tile([P, D, PACK], BF16, align_bytes=64)
        w2_codes = sbuf.tile([P, D], U32, align_bytes=64)
        w2_scales = sbuf.tile([P, D], U8, align_bytes=64)

        def regroup_w2(first):
            regroup(
                nc, w2_grouped[:, first : first + PIECE, :], w2_raw[:, :, first : first + PIECE]
            )

        def quantise_w2(first):
            quantise(
                nc,
                w2_codes[:, first : first + PIECE],
                w2_scales[:, first : first + PIECE],
                w2_grouped[:, first : first + PIECE, :].rearrange("p w j -> p (w j)"),
            )

        regroup_w2(0)
        bias_t = sbuf.tile([P, CHUNKS_1 + CHUNKS_2], F32)
        nc.scalar.copy(out=bias_t[:], in_=bias_ps[:, 0 : CHUNKS_1 + CHUNKS_2])
        a_t = sbuf.tile([P, CHUNKS_1, ROWS], F32)
        for c in range(CHUNKS_1):
            nc.scalar.activation(
                out=a_t[:, c, :], in_=a_ps[c][:], func=SILU, bias=bias_t[:, c : c + 1], scale=1.0
            )
        regroup_w2(PIECE)
        quantise_w2(0)
        h_grouped = sbuf.tile([P, 2, E * PACK], BF16, align_bytes=64)
        for half in range(2):
            nc.vector.tensor_tensor(
                out=h_grouped[:, half, :].rearrange("p (e s b) -> p e s b", s=2, b=2),
                in0=a_t[:, :, half * E : (half + 1) * E].rearrange("p (s b) e -> p e s b", b=2),
                in1=gate_ps[:].rearrange("p b e s -> p e s b"),
                op=MULT,
            )
        h_codes = sbuf.tile([P, ROWS], U32, align_bytes=64)
        h_scales = sbuf.tile([P, ROWS], U8, align_bytes=64)
        quantise(nc, h_codes[:], h_scales[:], h_grouped[:].rearrange("p half f -> p (half f)"))
        quantise_w2(PIECE)

        y_t = sbuf.tile([P, 2, CHUNKS_2, E], F32)

        def layer_2_chunk(c):
            y_ps = psum.tile([P, ROWS], F32, tag="bank")
            nc.tensor.matmul_mx(
                out=y_ps[:],
                lhsT=w2_codes[:, c * P : (c + 1) * P].bitcast(FP8X4),
                lhsT_scale=w2_scales[:, c * P : (c + 1) * P],
                rhs=h_codes[:].bitcast(FP8X4),
                rhs_scale=h_scales[:],
                start=True,
                stop=True,
            )
            nc.scalar.activation(
                out=y_t[:, :, c, :],
                in_=y_ps[:].rearrange("p (half e) -> p half e", half=2),
                func=SILU,
                bias=bias_t[:, CHUNKS_1 + c : CHUNKS_1 + c + 1],
                scale=1.0,
            )

        out_sb = sbuf.tile([P, PAIRS, P], F32)
        out_rows = out.rearrange("e (pair i) d -> i e pair d", i=2)

        def close_pair(pair):
            out_ps = psum.tile([P, P], F32, tag="bank")
            for half in range(2):
                nc.tensor.matmul(
                    out=out_ps[:],
                    lhsT=y_t[:, half, 2 * pair : 2 * pair + 2, :].rearrange("p c e -> p (c e)"),
                    rhs=ident_f32[:],
                    start=(half == 0),
                    stop=(half == 1),
                    is_transpose=True,
                )
            nc.vector.tensor_copy(out=out_sb[:, pair, :], in_=out_ps[:])
            if pair % 2 == 1:
                done = slice(pair - 1, pair + 1)
                for i in range(2):
                    nc.sync.dma_start(
                        out=out_rows[i][:, done, :], in_=out_sb[i * E : (i + 1) * E, done, :]
                    )

        for step in range(PAIRS + LAG):
            if step < PAIRS:
                layer_2_chunk(2 * step)
                layer_2_chunk(2 * step + 1)
            if step >= LAG:
                close_pair(step - LAG)
